import numpy as np
import ml_dtypes


def mxq(x, axis, fmt="e4m3"):
    dtype, down = {"e4m3": (ml_dtypes.float8_e4m3fn, 7), "e5m2": (ml_dtypes.float8_e5m2, 14)}[fmt]
    v = np.moveaxis(np.asarray(x, np.float32).astype(ml_dtypes.bfloat16).astype(np.float64), axis, -1)
    blocks = v.reshape(v.shape[:-1] + (-1, 32))
    amax = np.abs(blocks).max(-1, keepdims=True)
    byte = np.maximum(np.where(amax > 0, np.frexp(amax)[1] - 1 + 127, 0) - down, 1)
    scale = np.exp2(byte - 127.0)
    codes = (blocks / scale).astype(np.float32).astype(dtype).astype(np.float64)
    return np.moveaxis((codes * scale).reshape(v.shape), -1, axis)


WIDE = False


def mx_kscale(k):
    if not WIDE:
        return np.ones(k)
    levels = np.array([10, -10, 5, -5, 0])
    a = np.random.permutation(np.resize(levels, k // 512 * 4)).reshape(k // 512, 4)
    idx = np.arange(k)
    return np.exp2(a[idx // 512, idx % 128 // 32])


BF16 = ml_dtypes.bfloat16


def bf(x):
    return np.asarray(x, np.float32).astype(BF16)


def f64(x):
    return np.asarray(x).astype(np.float64)


E2M1 = np.array([0.0, 0.5, 1.0, 1.5, 2.0, 3.0, 4.0, 6.0, -0.0, -0.5, -1.0, -1.5, -2.0, -3.0, -4.0, -6.0])


def pack_weight(w, fmt):
    k, n = w.shape
    w = f64(bf(w)).reshape(k // 32, 32, n)
    amax = np.abs(w).max(1)
    if fmt == "e4m3":
        byte = np.frexp(amax)[1] - 1 + 127 - 7
    else:
        mant, ex = np.frexp(amax / 6.0)
        byte = np.where(mant > 0.5, ex, ex - 1) + 127
    byte = np.clip(np.where(amax > 0, byte, 1), 1, 254)
    scaled = (w * np.exp2(127.0 - byte)[:, None, :]).reshape(k, n).astype(np.float32)
    by_word = np.ascontiguousarray(scaled.reshape(k // 512, 128, 4, n).transpose(0, 1, 3, 2))
    if fmt == "e4m3":
        words = by_word.astype(ml_dtypes.float8_e4m3fn).view(np.uint8)
    else:
        c = by_word.astype(ml_dtypes.float4_e2m1fn).view(np.uint8) & 0xF
        words = c[..., 0::2] | (c[..., 1::2] << 4)
    return np.ascontiguousarray(words), np.ascontiguousarray(byte.astype(np.uint8).reshape(k // 512, 16, n))


def unpack_weight(words, scales, fmt):
    g, p, n, _ = words.shape
    if fmt == "e4m3":
        vals = np.ascontiguousarray(words).view(ml_dtypes.float8_e4m3fn).astype(np.float64)
    else:
        nib = np.empty((g, p, n, 4), np.uint8)
        nib[..., 0::2] = words & 0xF
        nib[..., 1::2] = words >> 4
        vals = E2M1[nib]
    vals = vals * np.repeat(np.exp2(scales.astype(np.float64) - 127.0), 8, axis=1)[..., None]
    return vals.transpose(0, 1, 3, 2).reshape(g * 512, n)

def pack4(w):
    words, scales = pack_weight(w, "e2m1")
    return words.reshape(words.shape[0], 128, -1), scales


def unpack4(words, scales):
    return unpack_weight(words.reshape(words.shape[0], 128, -1, 2), scales, "e2m1")


B, HEAD, NUM_EXPERTS, HEAD_DIM = 512, 4, 3, 512
EPS = 1e-5
VAR0 = 3e-4


def setup_inputs():
    s = mx_kscale(HEAD_DIM)
    p = (HEAD, NUM_EXPERTS, HEAD_DIM)

    def draw_x():
        return bf((np.random.standard_normal((B, HEAD, HEAD_DIM)) * s).reshape(B, HEAD * HEAD_DIM))

    x1 = draw_x()
    x2 = draw_x()
    x3 = draw_x()
    W = np.random.standard_normal((HEAD, NUM_EXPERTS, HEAD_DIM, HEAD_DIM)) / np.sqrt(HEAD_DIM) / s
    cat = np.ascontiguousarray(np.swapaxes(W, -1, -2)).reshape(-1, HEAD_DIM)
    words, scales = pack4(cat)
    return {"x1": x1, "x2": x2, "x3": x3,
            "W_words": words, "W_scales": scales,
            "b": bf(np.random.standard_normal(p) * 0.3),
            "gamma": bf(np.sqrt(VAR0) * (1.0 + 0.1 * np.random.standard_normal(p))),
            "beta": bf(np.random.standard_normal(p) * 0.3),
            "running_mean": bf(np.random.standard_normal(p) * 0.3),
            "running_var": bf(VAR0 * np.random.uniform(0.5, 1.5, p))}


def reference(x1, x2, x3, W_words, W_scales, b, gamma, beta, running_mean, running_var):
    n = x1.shape[0]
    xs = np.stack([f64(x1).reshape(n, HEAD, HEAD_DIM),
                   f64(x2).reshape(n, HEAD, HEAD_DIM),
                   f64(x3).reshape(n, HEAD, HEAD_DIM)], axis=2)
    xq = mxq(xs, 3, "e4m3")
    wt = unpack4(W_words, W_scales).reshape(HEAD, NUM_EXPERTS, HEAD_DIM, HEAD_DIM)
    y = (xq.transpose(1, 2, 0, 3) @ wt).transpose(2, 0, 1, 3) + f64(b)
    y = y * (1.0 / (1.0 + np.exp(-1.702 * y)))
    y = (y - f64(running_mean)) * (1.0 / np.sqrt(f64(running_var) + EPS)) * f64(gamma) + f64(beta)
    return np.transpose(y, (0, 2, 1, 3)).reshape(n, NUM_EXPERTS * HEAD * HEAD_DIM)

@@ -1,0 +1,242 @@
+from contextlib import ExitStack
+
+import concourse.mybir as mybir
+from concourse.masks import make_identity
+
+F32 = mybir.dt.float32
+BF16 = mybir.dt.bfloat16
+I32 = mybir.dt.int32
+U32 = mybir.dt.uint32
+U8 = mybir.dt.uint8
+FP8X4 = mybir.dt.float8_e4m3fn_x4
+FP4X4 = mybir.dt.float4_e2m1fn_x4
+ACT = mybir.ActivationFunctionType
+ALU = mybir.AluOpType
+
+P = 128
+TOKENS = 512
+TOKEN_TILES = TOKENS // P
+HEADS = 4
+EXPERTS = 3
+WIDTH = 512
+UNITS = HEADS * EXPERTS
+EPS = 1e-5
+
+FEATURE_BLOCKS = WIDTH // P
+BLOCKS_PER_ROUND = 2
+ROUNDS_PER_UNIT = FEATURE_BLOCKS // BLOCKS_PER_ROUND
+ROUNDS = UNITS * ROUNDS_PER_UNIT
+ROUND_FEATURES = BLOCKS_PER_ROUND * P
+ROUND_TOKEN_TILES = TOKEN_TILES // ROUNDS_PER_UNIT
+ROUND_TOKENS = ROUND_TOKEN_TILES * P
+
+QUANTISE_LAG = 1
+MATMUL_LAG = 3
+OUTPUT_LAG = 5
+
+FLOPS = 2 * TOKENS * WIDTH * WIDTH * UNITS
+
+
+def tile_mom_e_kernel(
+    tc, x1, x2, x3, W_words, W_scales, b, gamma, beta, running_mean, running_var, out
+):
+    nc = tc.nc
+    with ExitStack() as ctx:
+        ctx.enter_context(tc.manual_schedule())
+        const = ctx.enter_context(tc.tile_pool(name="const", bufs=1))
+        x_stage = ctx.enter_context(tc.tile_pool(name="x_stage", bufs=3))
+        z_pool = ctx.enter_context(tc.tile_pool(name="z_pool", bufs=4))
+        out_pool = ctx.enter_context(tc.tile_pool(name="out_pool", bufs=4))
+        psum_x = ctx.enter_context(tc.psum_pool(name="psum_x", bufs=2))
+        psum_acc = ctx.enter_context(tc.psum_pool(name="psum_acc", bufs=3))
+        psum_out = ctx.enter_context(tc.psum_pool(name="psum_out", bufs=3))
+
+        xs = [x1, x2, x3]
+        x_sb = []
+        for e in range(EXPERTS):
+            x_tile = const.tile([P, TOKEN_TILES, HEADS * WIDTH], BF16, name="x_sb%d" % e)
+            x_sb.append(x_tile)
+        x_dram = [x.rearrange("(p j) k -> p j k", j=TOKEN_TILES) for x in xs]
+
+        w_words = const.tile([P, EXPERTS, HEADS, 2 * WIDTH], U8, align_bytes=64)
+        w_planes = const.tile([P, UNITS, WIDTH], U8, align_bytes=64)
+        w_words_dram = W_words.bitcast(I32).rearrange("(h e) p w -> e p h w", e=EXPERTS)
+        w_scales_dram = W_scales.bitcast(I32).rearrange("g (q r) n -> r q g n", r=4)
+
+        vectors = [b, gamma, beta, running_mean, running_var]
+        VECTOR_ROWS = 16
+        ROW_BLOCKS = UNITS * FEATURE_BLOCKS // VECTOR_ROWS
+        rows = const.tile([P, ROW_BLOCKS, P], BF16)
+        nc.vector.memset(rows[:], 0.0)
+        nc.vector.memset(w_planes[:].bitcast(I32), 0)
+        for v in range(len(vectors)):
+            nc.scalar.dma_start(
+                out=rows[VECTOR_ROWS * v : VECTOR_ROWS * (v + 1)].rearrange("p a c -> p (a c)"),
+                in_=vectors[v]
+                .rearrange("h e f -> h (e f)")
+                .rearrange("h (q c) -> (h q) c", c=ROW_BLOCKS * P),
+            )
+
+        def load_x_head(e, h):
+            cols = slice(WIDTH * h, WIDTH * (h + 1))
+            nc.sync.dma_start(out=x_sb[e][:, :, cols], in_=x_dram[e][:, :, cols])
+
+        def load_weights(e):
+            nc.sync.dma_start(out=w_words[:, e].bitcast(I32), in_=w_words_dram[e])
+
+        load_x_head(0, 0)
+        load_x_head(0, 1)
+        load_weights(0)
+        for r in range(4):
+            nc.sync.dma_start(out=w_planes[:].bitcast(I32)[r:P:32], in_=w_scales_dram[r])
+        load_x_head(0, 2)
+        load_x_head(0, 3)
+        for e in range(1, EXPERTS):
+            load_weights(e)
+            nc.sync.dma_start(out=x_sb[e][:], in_=x_dram[e])
+
+        ident_f32 = const.tile([P, P], F32)
+        make_identity(nc, ident_f32[:])
+        ident_bf16 = const.tile([P, P], BF16)
+        nc.vector.tensor_copy(out=ident_bf16[:], in_=ident_f32[:])
+
+        rows_t = psum_x.tile([P, ROW_BLOCKS, P], BF16, tag="xt")
+        for a in range(ROW_BLOCKS):
+            nc.tensor.transpose(rows_t[:, a, :], rows[:, a, :], ident_bf16[:])
+        per_feature = const.tile([P, len(vectors), VECTOR_ROWS, ROW_BLOCKS], F32)
+        nc.vector.tensor_copy(
+            out=per_feature[:],
+            in_=rows_t[:, :, 0 : VECTOR_ROWS * len(vectors)].rearrange(
+                "p a (v q) -> p v q a", v=len(vectors)
+            ),
+        )
+        bias_t, gamma_t, beta_t, mean_t, var_t = [
+            per_feature[:, v].rearrange("p q a -> p (q a)") for v in range(len(vectors))
+        ]
+        BLOCKS = UNITS * FEATURE_BLOCKS
+        std = const.tile([P, BLOCKS], F32)
+        gain = const.tile([P, BLOCKS], F32)
+        shift = const.tile([P, BLOCKS], F32)
+        nc.vector.tensor_scalar_add(out=std[:], in0=var_t, scalar1=EPS)
+        nc.scalar.sqrt(out=std[:], in_=std[:])
+        nc.vector.reciprocal(out=gain[:], in_=std[:])
+        nc.vector.tensor_mul(out=gain[:], in0=gain[:], in1=gamma_t)
+        nc.vector.tensor_mul(out=shift[:], in0=mean_t, in1=gain[:])
+        nc.vector.tensor_sub(out=shift[:], in0=beta_t, in1=shift[:])
+
+        grouped = {}
+        codes = {}
+        x_planes = {}
+        z_tiles = {}
+        out_tiles = {}
+        out_dram = out.rearrange("(p j) n -> p j n", j=TOKEN_TILES)
+
+        def transpose_x(r):
+            unit, half = divmod(r, ROUNDS_PER_UNIT)
+            e, h = divmod(unit, HEADS)
+            x_words = x_sb[e][:].bitcast(F32)
+            xt = psum_x.tile([P, ROUND_TOKEN_TILES, 2, P], F32, tag="xt")
+            for jj in range(ROUND_TOKEN_TILES):
+                j = ROUND_TOKEN_TILES * half + jj
+                for u in range(2):
+                    first = (WIDTH // 2) * h + u
+                    nc.tensor.transpose(
+                        xt[:, jj, u, :],
+                        x_words[:, j, first : (WIDTH // 2) * (h + 1) : 2],
+                        ident_f32[:],
+                    )
+            if half == 0:
+                g = x_stage.tile([P, TOKEN_TILES, P, 4], BF16, align_bytes=64)
+                grouped[unit] = g
+            first_tile = ROUND_TOKEN_TILES * half
+            nc.vector.tensor_copy(
+                out=grouped[unit][:].bitcast(F32)[:, first_tile : first_tile + ROUND_TOKEN_TILES],
+                in_=xt[:].rearrange("p j u t -> p j t u"),
+            )
+
+        def quantise_x(r):
+            unit, half = divmod(r, ROUNDS_PER_UNIT)
+            if half == 0:
+                c = x_stage.tile([P, TOKENS], U32, align_bytes=64)
+                s = x_stage.tile([P, TOKENS], U8, align_bytes=64)
+                codes[unit] = c
+                x_planes[unit] = s
+            first_tile = ROUND_TOKEN_TILES * half
+            cols = slice(ROUND_TOKENS * half, ROUND_TOKENS * (half + 1))
+            nc.vector.quantize_mx(
+                out=codes[unit][:, cols].bitcast(FP8X4),
+                scales=x_planes[unit][:, cols],
+                in_=grouped[unit][:, first_tile : first_tile + ROUND_TOKEN_TILES].rearrange(
+                    "p j t k -> p (j t k)"
+                ),
+            )
+
+        def multiply(r):
+            unit, half = divmod(r, ROUNDS_PER_UNIT)
+            e, h = divmod(unit, HEADS)
+            group = EXPERTS * h + e
+            z = z_pool.tile([P, BLOCKS_PER_ROUND, TOKENS], F32)
+            z_tiles[r] = z
+            for i in range(BLOCKS_PER_ROUND):
+                block = BLOCKS_PER_ROUND * half + i
+                acc = psum_acc.tile([P, TOKENS], F32)
+                nc.tensor.matmul_mx(
+                    out=acc[:],
+                    lhsT=w_words[:, e, h, 2 * P * block : 2 * P * (block + 1)].bitcast(FP4X4),
+                    lhsT_scale=w_planes[:, group, P * block : P * (block + 1)],
+                    rhs=codes[unit][:].bitcast(FP8X4),
+                    rhs_scale=x_planes[unit][:],
+                    start=True,
+                    stop=True,
+                )
+                col = FEATURE_BLOCKS * group + block
+                nc.scalar.activation(
+                    out=z[:, i, :],
+                    in_=acc[:],
+                    func=ACT.Gelu_apprx_sigmoid,
+                    bias=bias_t[:, col : col + 1],
+                    scale=1.0,
+                )
+                nc.gpsimd.tensor_scalar(
+                    out=z[:, i, :],
+                    in0=z[:, i, :],
+                    scalar1=gain[:, col : col + 1],
+                    scalar2=shift[:, col : col + 1],
+                    op0=ALU.mult,
+                    op1=ALU.add,
+                )
+
+        def transpose_out(r):
+            unit, half = divmod(r, ROUNDS_PER_UNIT)
+            if half == 0:
+                o = out_pool.tile([P, TOKEN_TILES, WIDTH], F32)
+                out_tiles[unit] = o
+            z = z_tiles[r]
+            cols = slice(ROUND_FEATURES * half, ROUND_FEATURES * (half + 1))
+            for pair in range(TOKEN_TILES // 2):
+                zt = psum_out.tile([P, 2, ROUND_FEATURES], F32)
+                for jj in range(2):
+                    j = 2 * pair + jj
+                    for i in range(BLOCKS_PER_ROUND):
+                        nc.tensor.transpose(
+                            zt[:, jj, P * i : P * (i + 1)], z[:, i, P * j : P * (j + 1)], ident_f32[:]
+                        )
+                dst = out_tiles[unit][:, 2 * pair : 2 * pair + 2, cols]
+                if pair == 0:
+                    nc.scalar.copy(out=dst, in_=zt[:])
+                else:
+                    nc.vector.tensor_copy(out=dst, in_=zt[:])
+            if half == ROUNDS_PER_UNIT - 1:
+                nc.sync.dma_start(
+                    out=out_dram[:, :, WIDTH * unit : WIDTH * (unit + 1)], in_=out_tiles[unit][:]
+                )
+
+        for step in range(ROUNDS + OUTPUT_LAG):
+            if 0 <= step - QUANTISE_LAG < ROUNDS:
+                quantise_x(step - QUANTISE_LAG)
+            if 0 <= step - MATMUL_LAG < ROUNDS:
+                multiply(step - MATMUL_LAG)
+            if 0 <= step - OUTPUT_LAG < ROUNDS:
+                transpose_out(step - OUTPUT_LAG)
+            if step < ROUNDS:
+                transpose_x(step)

@@ -23,16 +23,11 @@ UNITS = HEADS * EXPERTS
 EPS = 1e-5
 
 FEATURE_BLOCKS = WIDTH // P
-BLOCKS_PER_ROUND = 2
-ROUNDS_PER_UNIT = FEATURE_BLOCKS // BLOCKS_PER_ROUND
-ROUNDS = UNITS * ROUNDS_PER_UNIT
-ROUND_FEATURES = BLOCKS_PER_ROUND * P
-ROUND_TOKEN_TILES = TOKEN_TILES // ROUNDS_PER_UNIT
-ROUND_TOKENS = ROUND_TOKEN_TILES * P
+BANK = 512
 
 QUANTISE_LAG = 1
-MATMUL_LAG = 3
-OUTPUT_LAG = 5
+MATMUL_LAG = 2
+OUTPUT_LAG = 3
 
 FLOPS = 2 * TOKENS * WIDTH * WIDTH * UNITS
 
@@ -45,11 +40,9 @@ def tile_mom_e_kernel(
         ctx.enter_context(tc.manual_schedule())
         const = ctx.enter_context(tc.tile_pool(name="const", bufs=1))
         x_stage = ctx.enter_context(tc.tile_pool(name="x_stage", bufs=3))
-        z_pool = ctx.enter_context(tc.tile_pool(name="z_pool", bufs=4))
-        out_pool = ctx.enter_context(tc.tile_pool(name="out_pool", bufs=4))
-        psum_x = ctx.enter_context(tc.psum_pool(name="psum_x", bufs=2))
-        psum_acc = ctx.enter_context(tc.psum_pool(name="psum_acc", bufs=3))
-        psum_out = ctx.enter_context(tc.psum_pool(name="psum_out", bufs=3))
+        z_pool = ctx.enter_context(tc.tile_pool(name="z_pool", bufs=3))
+        out_pool = ctx.enter_context(tc.tile_pool(name="out_pool", bufs=3))
+        psum = ctx.enter_context(tc.psum_pool(name="psum", bufs=8))
 
         xs = [x1, x2, x3]
         x_sb = []
@@ -100,7 +93,7 @@ def tile_mom_e_kernel(
         ident_bf16 = const.tile([P, P], BF16)
         nc.vector.tensor_copy(out=ident_bf16[:], in_=ident_f32[:])
 
-        rows_t = psum_x.tile([P, ROW_BLOCKS, P], BF16, tag="xt")
+        rows_t = psum.tile([P, ROW_BLOCKS, P], BF16, tag="bank")
         for a in range(ROW_BLOCKS):
             nc.tensor.transpose(rows_t[:, a, :], rows[:, a, :], ident_bf16[:])
         per_feature = const.tile([P, len(vectors), VECTOR_ROWS, ROW_BLOCKS], F32)
@@ -128,58 +121,48 @@ def tile_mom_e_kernel(
         codes = {}
         x_planes = {}
         z_tiles = {}
-        out_tiles = {}
         out_dram = out.rearrange("(p j) n -> p j n", j=TOKEN_TILES)
 
-        def transpose_x(r):
-            unit, half = divmod(r, ROUNDS_PER_UNIT)
+        def transpose_x(unit):
             e, h = divmod(unit, HEADS)
             x_words = x_sb[e][:].bitcast(F32)
-            xt = psum_x.tile([P, ROUND_TOKEN_TILES, 2, P], F32, tag="xt")
-            for jj in range(ROUND_TOKEN_TILES):
-                j = ROUND_TOKEN_TILES * half + jj
-                for u in range(2):
-                    first = (WIDTH // 2) * h + u
-                    nc.tensor.transpose(
-                        xt[:, jj, u, :],
-                        x_words[:, j, first : (WIDTH // 2) * (h + 1) : 2],
-                        ident_f32[:],
-                    )
-            if half == 0:
-                g = x_stage.tile([P, TOKEN_TILES, P, 4], BF16, align_bytes=64)
-                grouped[unit] = g
-            first_tile = ROUND_TOKEN_TILES * half
-            nc.vector.tensor_copy(
-                out=grouped[unit][:].bitcast(F32)[:, first_tile : first_tile + ROUND_TOKEN_TILES],
-                in_=xt[:].rearrange("p j u t -> p j t u"),
-            )
+            g = x_stage.tile([P, TOKEN_TILES, P, 4], BF16, align_bytes=64)
+            grouped[unit] = g
+            for pair in range(TOKEN_TILES // 2):
+                xt = psum.tile([P, 2, 2, P], F32, tag="bank")
+                for jj in range(2):
+                    for u in range(2):
+                        first = (WIDTH // 2) * h + u
+                        nc.tensor.transpose(
+                            xt[:, jj, u, :],
+                            x_words[:, 2 * pair + jj, first : (WIDTH // 2) * (h + 1) : 2],
+                            ident_f32[:],
+                        )
+                nc.vector.tensor_copy(
+                    out=g[:].bitcast(F32)[:, 2 * pair : 2 * pair + 2],
+                    in_=xt[:].rearrange("p j u t -> p j t u"),
+                )
 
-        def quantise_x(r):
-            unit, half = divmod(r, ROUNDS_PER_UNIT)
-            if half == 0:
-                c = x_stage.tile([P, TOKENS], U32, align_bytes=64)
-                s = x_stage.tile([P, TOKENS], U8, align_bytes=64)
-                codes[unit] = c
-                x_planes[unit] = s
-            first_tile = ROUND_TOKEN_TILES * half
-            cols = slice(ROUND_TOKENS * half, ROUND_TOKENS * (half + 1))
+        def quantise_x(unit):
+            c = x_stage.tile([P, TOKENS], U32, align_bytes=64)
+            s = x_stage.tile([P, TOKENS], U8, align_bytes=64)
+            codes[unit] = c
+            x_planes[unit] = s
             nc.vector.quantize_mx(
-                out=codes[unit][:, cols].bitcast(FP8X4),
-                scales=x_planes[unit][:, cols],
-                in_=grouped[unit][:, first_tile : first_tile + ROUND_TOKEN_TILES].rearrange(
-                    "p j t k -> p (j t k)"
-                ),
+                out=c[:].bitcast(FP8X4),
+                scales=s[:],
+                in_=grouped[unit][:].rearrange("p j t k -> p (j t k)"),
             )
 
-        def multiply(r):
-            unit, half = divmod(r, ROUNDS_PER_UNIT)
+        def multiply(unit):
             e, h = divmod(unit, HEADS)
             group = EXPERTS * h + e
-            z = z_pool.tile([P, BLOCKS_PER_ROUND, TOKENS], F32)
-            z_tiles[r] = z
-            for i in range(BLOCKS_PER_ROUND):
-                block = BLOCKS_PER_ROUND * half + i
-                acc = psum_acc.tile([P, TOKENS], F32)
+            z = z_pool.tile([P, FEATURE_BLOCKS, TOKENS], F32)
+            z_tiles[unit] = z
+            accs = []
+            for block in range(FEATURE_BLOCKS):
+                acc = psum.tile([P, TOKENS], F32, tag="bank")
+                accs.append(acc)
                 nc.tensor.matmul_mx(
                     out=acc[:],
                     lhsT=w_words[:, e, h, 2 * P * block : 2 * P * (block + 1)].bitcast(FP4X4),
@@ -189,54 +172,52 @@ def tile_mom_e_kernel(
                     start=True,
                     stop=True,
                 )
+            for block in range(FEATURE_BLOCKS):
                 col = FEATURE_BLOCKS * group + block
                 nc.scalar.activation(
-                    out=z[:, i, :],
-                    in_=acc[:],
+                    out=z[:, block, :],
+                    in_=accs[block][:],
                     func=ACT.Gelu_apprx_sigmoid,
                     bias=bias_t[:, col : col + 1],
                     scale=1.0,
                 )
                 nc.gpsimd.tensor_scalar(
-                    out=z[:, i, :],
-                    in0=z[:, i, :],
+                    out=z[:, block, :],
+                    in0=z[:, block, :],
                     scalar1=gain[:, col : col + 1],
                     scalar2=shift[:, col : col + 1],
                     op0=ALU.mult,
                     op1=ALU.add,
                 )
 
-        def transpose_out(r):
-            unit, half = divmod(r, ROUNDS_PER_UNIT)
-            if half == 0:
-                o = out_pool.tile([P, TOKEN_TILES, WIDTH], F32)
-                out_tiles[unit] = o
-            z = z_tiles[r]
-            cols = slice(ROUND_FEATURES * half, ROUND_FEATURES * (half + 1))
-            for pair in range(TOKEN_TILES // 2):
-                zt = psum_out.tile([P, 2, ROUND_FEATURES], F32)
-                for jj in range(2):
-                    j = 2 * pair + jj
-                    for i in range(BLOCKS_PER_ROUND):
-                        nc.tensor.transpose(
-                            zt[:, jj, P * i : P * (i + 1)], z[:, i, P * j : P * (j + 1)], ident_f32[:]
-                        )
-                dst = out_tiles[unit][:, 2 * pair : 2 * pair + 2, cols]
-                if pair == 0:
-                    nc.scalar.copy(out=dst, in_=zt[:])
-                else:
-                    nc.vector.tensor_copy(out=dst, in_=zt[:])
-            if half == ROUNDS_PER_UNIT - 1:
-                nc.sync.dma_start(
-                    out=out_dram[:, :, WIDTH * unit : WIDTH * (unit + 1)], in_=out_tiles[unit][:]
-                )
+        def transpose_out(unit):
+            o = out_pool.tile([P, TOKEN_TILES, WIDTH], F32)
+            z = z_tiles[unit]
+            scalar_banks = (2, 3) if unit % 2 == 0 else (3,)
+            for half in range(2):
+                for pair in range(TOKEN_TILES // 2):
+                    zt = psum.tile([P, 2, BANK // 2], F32, tag="bank")
+                    for jj in range(2):
+                        j = 2 * pair + jj
+                        for i in range(2):
+                            nc.tensor.transpose(
+                                zt[:, jj, P * i : P * (i + 1)],
+                                z[:, 2 * half + i, P * j : P * (j + 1)],
+                                ident_f32[:],
+                            )
+                    dst = o[:, 2 * pair : 2 * pair + 2, (BANK // 2) * half : (BANK // 2) * (half + 1)]
+                    if 2 * half + pair in scalar_banks:
+                        nc.scalar.copy(out=dst, in_=zt[:])
+                    else:
+                        nc.vector.tensor_copy(out=dst, in_=zt[:])
+            nc.sync.dma_start(out=out_dram[:, :, WIDTH * unit : WIDTH * (unit + 1)], in_=o[:])
 
-        for step in range(ROUNDS + OUTPUT_LAG):
-            if 0 <= step - QUANTISE_LAG < ROUNDS:
+        for step in range(UNITS + OUTPUT_LAG):
+            if 0 <= step - QUANTISE_LAG < UNITS:
                 quantise_x(step - QUANTISE_LAG)
-            if 0 <= step - MATMUL_LAG < ROUNDS:
+            if 0 <= step - MATMUL_LAG < UNITS:
                 multiply(step - MATMUL_LAG)
-            if 0 <= step - OUTPUT_LAG < ROUNDS:
+            if 0 <= step - OUTPUT_LAG < UNITS:
                 transpose_out(step - OUTPUT_LAG)
-            if step < ROUNDS:
+            if step < UNITS:
                 transpose_x(step)

@@ -25,9 +25,7 @@ EPS = 1e-5
 FEATURE_BLOCKS = WIDTH // P
 BANK = 512
 
-QUANTISE_LAG = 1
-MATMUL_LAG = 2
-OUTPUT_LAG = 3
+X_AHEAD = 2
 
 FLOPS = 2 * TOKENS * WIDTH * WIDTH * UNITS
 
@@ -46,8 +44,8 @@ def tile_mom_e_kernel(
 
         xs = [x1, x2, x3]
         x_sb = []
-        for e in range(EXPERTS):
-            x_tile = const.tile([P, TOKEN_TILES, HEADS * WIDTH], BF16, name="x_sb%d" % e)
+        for unit in range(UNITS):
+            x_tile = const.tile([P, TOKEN_TILES, WIDTH], BF16, name="x_sb%d" % unit)
             x_sb.append(x_tile)
         x_dram = [x.rearrange("(p j) k -> p j k", j=TOKEN_TILES) for x in xs]
 
@@ -70,52 +68,57 @@ def tile_mom_e_kernel(
                 .rearrange("h (q c) -> (h q) c", c=ROW_BLOCKS * P),
             )
 
-        def load_x_head(e, h):
-            cols = slice(WIDTH * h, WIDTH * (h + 1))
-            nc.sync.dma_start(out=x_sb[e][:, :, cols], in_=x_dram[e][:, :, cols])
+        def load_x(unit):
+            e, h = divmod(unit, HEADS)
+            nc.sync.dma_start(out=x_sb[unit][:], in_=x_dram[e][:, :, WIDTH * h : WIDTH * (h + 1)])
 
         def load_weights(e):
             nc.sync.dma_start(out=w_words[:, e].bitcast(I32), in_=w_words_dram[e])
 
-        load_x_head(0, 0)
-        load_x_head(0, 1)
+        load_x(0)
         load_weights(0)
         for r in range(4):
             nc.sync.dma_start(out=w_planes[:].bitcast(I32)[r:P:32], in_=w_scales_dram[r])
-        load_x_head(0, 2)
-        load_x_head(0, 3)
-        for e in range(1, EXPERTS):
-            load_weights(e)
-            nc.sync.dma_start(out=x_sb[e][:], in_=x_dram[e])
+        for e in range(EXPERTS):
+            if e > 0:
+                load_weights(e)
+            for h in range(HEADS):
+                if HEADS * e + h > 0:
+                    load_x(HEADS * e + h)
 
         ident_f32 = const.tile([P, P], F32)
         make_identity(nc, ident_f32[:])
         ident_bf16 = const.tile([P, P], BF16)
-        nc.vector.tensor_copy(out=ident_bf16[:], in_=ident_f32[:])
+        make_identity(nc, ident_bf16[:])
 
-        rows_t = psum.tile([P, ROW_BLOCKS, P], BF16, tag="bank")
-        for a in range(ROW_BLOCKS):
-            nc.tensor.transpose(rows_t[:, a, :], rows[:, a, :], ident_bf16[:])
-        per_feature = const.tile([P, len(vectors), VECTOR_ROWS, ROW_BLOCKS], F32)
-        nc.vector.tensor_copy(
-            out=per_feature[:],
-            in_=rows_t[:, :, 0 : VECTOR_ROWS * len(vectors)].rearrange(
-                "p a (v q) -> p v q a", v=len(vectors)
-            ),
-        )
-        bias_t, gamma_t, beta_t, mean_t, var_t = [
-            per_feature[:, v].rearrange("p q a -> p (q a)") for v in range(len(vectors))
-        ]
         BLOCKS = UNITS * FEATURE_BLOCKS
-        std = const.tile([P, BLOCKS], F32)
+        per_feature = const.tile([P, 4, VECTOR_ROWS, ROW_BLOCKS], F32)
+        std = const.tile([P, VECTOR_ROWS, ROW_BLOCKS], F32)
         gain = const.tile([P, BLOCKS], F32)
         shift = const.tile([P, BLOCKS], F32)
-        nc.vector.tensor_scalar_add(out=std[:], in0=var_t, scalar1=EPS)
-        nc.scalar.sqrt(out=std[:], in_=std[:])
-        nc.vector.reciprocal(out=gain[:], in_=std[:])
-        nc.vector.tensor_mul(out=gain[:], in0=gain[:], in1=gamma_t)
-        nc.vector.tensor_mul(out=shift[:], in0=mean_t, in1=gain[:])
-        nc.vector.tensor_sub(out=shift[:], in0=beta_t, in1=shift[:])
+        bias_t, gamma_t, beta_t, mean_t = [
+            per_feature[:, v].rearrange("p q a -> p (q a)") for v in range(4)
+        ]
+
+        def per_feature_constants():
+            rows_t = psum.tile([P, ROW_BLOCKS, P], BF16, tag="bank")
+            for a in range(ROW_BLOCKS):
+                nc.tensor.transpose(rows_t[:, a, :], rows[:, a, :], ident_bf16[:])
+            nc.scalar.activation(
+                out=std[:],
+                in_=rows_t[:, :, 4 * VECTOR_ROWS : 5 * VECTOR_ROWS].rearrange("p a q -> p q a"),
+                func=ACT.Sqrt,
+                bias=EPS,
+                scale=1.0,
+            )
+            nc.scalar.copy(
+                out=per_feature[:],
+                in_=rows_t[:, :, 0 : 4 * VECTOR_ROWS].rearrange("p a (v q) -> p v q a", v=4),
+            )
+            nc.vector.reciprocal(out=gain[:], in_=std[:].rearrange("p q a -> p (q a)"))
+            nc.vector.tensor_mul(out=gain[:], in0=gain[:], in1=gamma_t)
+            nc.vector.tensor_mul(out=shift[:], in0=mean_t, in1=gain[:])
+            nc.vector.tensor_sub(out=shift[:], in0=beta_t, in1=shift[:])
 
         grouped = {}
         codes = {}
@@ -124,19 +127,15 @@ def tile_mom_e_kernel(
         out_dram = out.rearrange("(p j) n -> p j n", j=TOKEN_TILES)
 
         def transpose_x(unit):
-            e, h = divmod(unit, HEADS)
-            x_words = x_sb[e][:].bitcast(F32)
+            x_words = x_sb[unit][:].bitcast(F32)
             g = x_stage.tile([P, TOKEN_TILES, P, 4], BF16, align_bytes=64)
             grouped[unit] = g
             for pair in range(TOKEN_TILES // 2):
                 xt = psum.tile([P, 2, 2, P], F32, tag="bank")
                 for jj in range(2):
                     for u in range(2):
-                        first = (WIDTH // 2) * h + u
                         nc.tensor.transpose(
-                            xt[:, jj, u, :],
-                            x_words[:, 2 * pair + jj, first : (WIDTH // 2) * (h + 1) : 2],
-                            ident_f32[:],
+                            xt[:, jj, u, :], x_words[:, 2 * pair + jj, u : WIDTH // 2 : 2], ident_f32[:]
                         )
                 nc.vector.tensor_copy(
                     out=g[:].bitcast(F32)[:, 2 * pair : 2 * pair + 2],
@@ -212,12 +211,22 @@ def tile_mom_e_kernel(
                         nc.vector.tensor_copy(out=dst, in_=zt[:])
             nc.sync.dma_start(out=out_dram[:, :, WIDTH * unit : WIDTH * (unit + 1)], in_=o[:])
 
-        for step in range(UNITS + OUTPUT_LAG):
-            if 0 <= step - QUANTISE_LAG < UNITS:
-                quantise_x(step - QUANTISE_LAG)
-            if 0 <= step - MATMUL_LAG < UNITS:
-                multiply(step - MATMUL_LAG)
-            if 0 <= step - OUTPUT_LAG < UNITS:
-                transpose_out(step - OUTPUT_LAG)
-            if step < UNITS:
-                transpose_x(step)
+        transpose_x(0)
+        quantise_x(0)
+        per_feature_constants()
+        transposed = 0
+        quantised = 0
+        for unit in range(UNITS):
+            if quantised < min(unit + 1, transposed):
+                quantised += 1
+                quantise_x(quantised)
+            multiply(unit)
+            while transposed < min(unit + X_AHEAD, UNITS - 1):
+                transposed += 1
+                transpose_x(transposed)
+                if quantised < min(unit + 1, transposed):
+                    quantised += 1
+                    quantise_x(quantised)
+            if unit > 0:
+                transpose_out(unit - 1)
+        transpose_out(UNITS - 1)

@@ -26,6 +26,7 @@ FEATURE_BLOCKS = WIDTH // P
 BANK = 512
 
 X_AHEAD = 2
+FINE_STORES = 2
 
 FLOPS = 2 * TOKENS * WIDTH * WIDTH * UNITS
 
@@ -180,7 +181,8 @@ def tile_mom_e_kernel(
                     bias=bias_t[:, col : col + 1],
                     scale=1.0,
                 )
-                nc.gpsimd.tensor_scalar(
+                engine = nc.vector if (block == 0 and unit % 2 == 1) else nc.gpsimd
+                engine.tensor_scalar(
                     out=z[:, block, :],
                     in0=z[:, block, :],
                     scalar1=gain[:, col : col + 1],
@@ -209,7 +211,14 @@ def tile_mom_e_kernel(
                         nc.scalar.copy(out=dst, in_=zt[:])
                     else:
                         nc.vector.tensor_copy(out=dst, in_=zt[:])
-            nc.sync.dma_start(out=out_dram[:, :, WIDTH * unit : WIDTH * (unit + 1)], in_=o[:])
+                if unit >= UNITS - FINE_STORES:
+                    first = (BANK // 2) * half
+                    nc.sync.dma_start(
+                        out=out_dram[:, :, WIDTH * unit + first : WIDTH * unit + first + BANK // 2],
+                        in_=o[:, :, first : first + BANK // 2],
+                    )
+            if unit < UNITS - FINE_STORES:
+                nc.sync.dma_start(out=out_dram[:, :, WIDTH * unit : WIDTH * (unit + 1)], in_=o[:])
 
         transpose_x(0)
         quantise_x(0)

@@ -25,7 +25,7 @@ EPS = 1e-5
 FEATURE_BLOCKS = WIDTH // P
 BANK = 512
 
-X_AHEAD = 2
+X_AHEAD = 3
 FINE_STORES = 2
 
 FLOPS = 2 * TOKENS * WIDTH * WIDTH * UNITS
@@ -38,9 +38,9 @@ def tile_mom_e_kernel(
     with ExitStack() as ctx:
         ctx.enter_context(tc.manual_schedule())
         const = ctx.enter_context(tc.tile_pool(name="const", bufs=1))
-        x_stage = ctx.enter_context(tc.tile_pool(name="x_stage", bufs=3))
-        z_pool = ctx.enter_context(tc.tile_pool(name="z_pool", bufs=3))
-        out_pool = ctx.enter_context(tc.tile_pool(name="out_pool", bufs=3))
+        x_stage = ctx.enter_context(tc.tile_pool(name="x_stage", bufs=5))
+        z_pool = ctx.enter_context(tc.tile_pool(name="z_pool", bufs=4))
+        out_pool = ctx.enter_context(tc.tile_pool(name="out_pool", bufs=4))
         psum = ctx.enter_context(tc.psum_pool(name="psum", bufs=8))
 
         xs = [x1, x2, x3]

@@ -25,7 +25,7 @@ EPS = 1e-5
 FEATURE_BLOCKS = WIDTH // P
 BANK = 512
 
-X_AHEAD = 3
+X_AHEAD = 2
 FINE_STORES = 2
 
 FLOPS = 2 * TOKENS * WIDTH * WIDTH * UNITS
@@ -51,16 +51,18 @@ def tile_mom_e_kernel(
         x_dram = [x.rearrange("(p j) k -> p j k", j=TOKEN_TILES) for x in xs]
 
         w_words = const.tile([P, EXPERTS, HEADS, 2 * WIDTH], U8, align_bytes=64)
-        w_planes = const.tile([P, UNITS, WIDTH], U8, align_bytes=64)
+        w_planes_first = const.tile([P, HEADS, WIDTH], U8, align_bytes=64)
+        w_planes_rest = const.tile([P, EXPERTS - 1, HEADS, WIDTH], U8, align_bytes=64)
+        w_planes = [w_planes_first[:], w_planes_rest[:, 0], w_planes_rest[:, 1]]
         w_words_dram = W_words.bitcast(I32).rearrange("(h e) p w -> e p h w", e=EXPERTS)
-        w_scales_dram = W_scales.bitcast(I32).rearrange("g (q r) n -> r q g n", r=4)
+        w_scales_dram = W_scales.bitcast(I32).rearrange("(h e) (q r) n -> e r q h n", e=EXPERTS, r=4)
 
-        vectors = [b, gamma, beta, running_mean, running_var]
+        vectors = [running_var, b, gamma, beta, running_mean]
         VECTOR_ROWS = 16
         ROW_BLOCKS = UNITS * FEATURE_BLOCKS // VECTOR_ROWS
         rows = const.tile([P, ROW_BLOCKS, P], BF16)
-        nc.vector.memset(rows[:], 0.0)
-        nc.vector.memset(w_planes[:].bitcast(I32), 0)
+        nc.vector.memset(rows[P // 2 : P], 0.0)
+        nc.vector.memset(w_planes_first[:].rearrange("p h n -> p (h n)").bitcast(I32), 0)
         for v in range(len(vectors)):
             nc.scalar.dma_start(
                 out=rows[VECTOR_ROWS * v : VECTOR_ROWS * (v + 1)].rearrange("p a c -> p (a c)"),
@@ -73,29 +75,37 @@ def tile_mom_e_kernel(
             e, h = divmod(unit, HEADS)
             nc.sync.dma_start(out=x_sb[unit][:], in_=x_dram[e][:, :, WIDTH * h : WIDTH * (h + 1)])
 
-        def load_weights(e):
-            nc.sync.dma_start(out=w_words[:, e].bitcast(I32), in_=w_words_dram[e])
+        def load_weights(e, h0, h1):
+            nc.sync.dma_start(
+                out=w_words[:, e, h0:h1].bitcast(I32), in_=w_words_dram[e][:, h0:h1]
+            )
 
-        load_x(0)
-        load_weights(0)
-        for r in range(4):
-            nc.sync.dma_start(out=w_planes[:].bitcast(I32)[r:P:32], in_=w_scales_dram[r])
-        for e in range(EXPERTS):
-            if e > 0:
-                load_weights(e)
-            for h in range(HEADS):
-                if HEADS * e + h > 0:
-                    load_x(HEADS * e + h)
+        def load_scales(e):
+            for r in range(4):
+                nc.sync.dma_start(out=w_planes[e].bitcast(I32)[r:P:32], in_=w_scales_dram[e][r])
 
         ident_f32 = const.tile([P, P], F32)
         make_identity(nc, ident_f32[:])
         ident_bf16 = const.tile([P, P], BF16)
         make_identity(nc, ident_bf16[:])
+        nc.gpsimd.memset(w_planes_rest[:].rearrange("p e h n -> p (e h n)").bitcast(I32), 0)
+
+        load_x(0)
+        load_weights(0, 0, 1)
+        load_scales(0)
+        load_x(1)
+        load_weights(0, 1, HEADS)
+        for unit in range(2, UNITS):
+            load_x(unit)
+            if unit % HEADS == 0:
+                load_weights(unit // HEADS, 0, HEADS)
+                load_scales(unit // HEADS)
 
         BLOCKS = UNITS * FEATURE_BLOCKS
         per_feature = const.tile([P, 4, VECTOR_ROWS, ROW_BLOCKS], F32)
         std = const.tile([P, VECTOR_ROWS, ROW_BLOCKS], F32)
         gain = const.tile([P, BLOCKS], F32)
+        table_probe = const.tile([P, 1], F32)
         shift = const.tile([P, BLOCKS], F32)
         bias_t, gamma_t, beta_t, mean_t = [
             per_feature[:, v].rearrange("p q a -> p (q a)") for v in range(4)
@@ -107,14 +117,17 @@ def tile_mom_e_kernel(
                 nc.tensor.transpose(rows_t[:, a, :], rows[:, a, :], ident_bf16[:])
             nc.scalar.activation(
                 out=std[:],
-                in_=rows_t[:, :, 4 * VECTOR_ROWS : 5 * VECTOR_ROWS].rearrange("p a q -> p q a"),
+                in_=rows_t[:, :, 0:VECTOR_ROWS].rearrange("p a q -> p q a"),
                 func=ACT.Sqrt,
                 bias=EPS,
                 scale=1.0,
             )
             nc.scalar.copy(
                 out=per_feature[:],
-                in_=rows_t[:, :, 0 : 4 * VECTOR_ROWS].rearrange("p a (v q) -> p v q a", v=4),
+                in_=rows_t[:, :, VECTOR_ROWS : 5 * VECTOR_ROWS].rearrange("p a (v q) -> p v q a", v=4),
+            )
+            nc.scalar.activation(
+                out=table_probe[:], in_=std[:, 0, 0:1], func=ACT.Gelu_apprx_sigmoid, scale=1.0
             )
             nc.vector.reciprocal(out=gain[:], in_=std[:].rearrange("p q a -> p (q a)"))
             nc.vector.tensor_mul(out=gain[:], in0=gain[:], in1=gamma_t)
@@ -166,7 +179,7 @@ def tile_mom_e_kernel(
                 nc.tensor.matmul_mx(
                     out=acc[:],
                     lhsT=w_words[:, e, h, 2 * P * block : 2 * P * (block + 1)].bitcast(FP4X4),
-                    lhsT_scale=w_planes[:, group, P * block : P * (block + 1)],
+                    lhsT_scale=w_planes[e][:, h, P * block : P * (block + 1)],
                     rhs=codes[unit][:].bitcast(FP8X4),
                     rhs_scale=x_planes[unit][:],
                     start=True,

@@ -91,19 +91,20 @@ def tile_mom_e_kernel(
         nc.gpsimd.memset(w_planes_rest[:].rearrange("p e h n -> p (e h n)").bitcast(I32), 0)
 
         load_x(0)
+        load_x(1)
         load_weights(0, 0, 1)
         load_scales(0)
-        load_x(1)
+        load_x(2)
         load_weights(0, 1, HEADS)
-        for unit in range(2, UNITS):
+        for unit in range(3, UNITS):
             load_x(unit)
-            if unit % HEADS == 0:
+            if unit > HEADS and unit % HEADS == 1:
                 load_weights(unit // HEADS, 0, HEADS)
                 load_scales(unit // HEADS)
 
         BLOCKS = UNITS * FEATURE_BLOCKS
         per_feature = const.tile([P, 4, VECTOR_ROWS, ROW_BLOCKS], F32)
-        std = const.tile([P, VECTOR_ROWS, ROW_BLOCKS], F32)
+        rstd = const.tile([P, VECTOR_ROWS, ROW_BLOCKS], F32)
         gain = const.tile([P, BLOCKS], F32)
         table_probe = const.tile([P, 1], F32)
         shift = const.tile([P, BLOCKS], F32)
@@ -116,9 +117,9 @@ def tile_mom_e_kernel(
             for a in range(ROW_BLOCKS):
                 nc.tensor.transpose(rows_t[:, a, :], rows[:, a, :], ident_bf16[:])
             nc.scalar.activation(
-                out=std[:],
+                out=rstd[:],
                 in_=rows_t[:, :, 0:VECTOR_ROWS].rearrange("p a q -> p q a"),
-                func=ACT.Sqrt,
+                func=ACT.Abs_reciprocal_sqrt,
                 bias=EPS,
                 scale=1.0,
             )
@@ -127,12 +128,11 @@ def tile_mom_e_kernel(
                 in_=rows_t[:, :, VECTOR_ROWS : 5 * VECTOR_ROWS].rearrange("p a (v q) -> p v q a", v=4),
             )
             nc.scalar.activation(
-                out=table_probe[:], in_=std[:, 0, 0:1], func=ACT.Gelu_apprx_sigmoid, scale=1.0
+                out=table_probe[:], in_=rstd[:, 0, 0:1], func=ACT.Gelu_apprx_sigmoid, scale=1.0
             )
-            nc.vector.reciprocal(out=gain[:], in_=std[:].rearrange("p q a -> p (q a)"))
-            nc.vector.tensor_mul(out=gain[:], in0=gain[:], in1=gamma_t)
-            nc.vector.tensor_mul(out=shift[:], in0=mean_t, in1=gain[:])
-            nc.vector.tensor_sub(out=shift[:], in0=beta_t, in1=shift[:])
+            nc.gpsimd.tensor_mul(out=gain[:], in0=rstd[:].rearrange("p q a -> p (q a)"), in1=gamma_t)
+            nc.gpsimd.tensor_mul(out=shift[:], in0=mean_t, in1=gain[:])
+            nc.gpsimd.tensor_sub(out=shift[:], in0=beta_t, in1=shift[:])
 
         grouped = {}
         codes = {}
@@ -236,7 +236,8 @@ def tile_mom_e_kernel(
         transpose_x(0)
         quantise_x(0)
         per_feature_constants()
-        transposed = 0
+        transposed = 1
+        transpose_x(1)
         quantised = 0
         for unit in range(UNITS):
             if quantised < min(unit + 1, transposed):

@@ -61,6 +61,8 @@ def tile_mom_e_kernel(
         VECTOR_ROWS = 16
         ROW_BLOCKS = UNITS * FEATURE_BLOCKS // VECTOR_ROWS
         rows = const.tile([P, ROW_BLOCKS, P], BF16)
+        warm = const.tile([P, BANK], BF16)
+        nc.vector.memset(warm[:], 0.0)
         nc.vector.memset(rows[P // 2 : P], 0.0)
         nc.vector.memset(w_planes_first[:].rearrange("p h n -> p (h n)").bitcast(I32), 0)
         for v in range(len(vectors)):
@@ -84,6 +86,11 @@ def tile_mom_e_kernel(
             for r in range(4):
                 nc.sync.dma_start(out=w_planes[e].bitcast(I32)[r:P:32], in_=w_scales_dram[e][r])
 
+        table_probe = const.tile([P, 1], F32)
+        nc.vector.memset(table_probe[:], 1.0)
+        nc.scalar.activation(
+            out=table_probe[:], in_=table_probe[:], func=ACT.Abs_reciprocal_sqrt, scale=1.0
+        )
         ident_f32 = const.tile([P, P], F32)
         make_identity(nc, ident_f32[:])
         ident_bf16 = const.tile([P, P], BF16)
@@ -106,7 +113,6 @@ def tile_mom_e_kernel(
         per_feature = const.tile([P, 4, VECTOR_ROWS, ROW_BLOCKS], F32)
         rstd = const.tile([P, VECTOR_ROWS, ROW_BLOCKS], F32)
         gain = const.tile([P, BLOCKS], F32)
-        table_probe = const.tile([P, 1], F32)
         shift = const.tile([P, BLOCKS], F32)
         bias_t, gamma_t, beta_t, mean_t = [
             per_feature[:, v].rearrange("p q a -> p (q a)") for v in range(4)
@@ -151,10 +157,12 @@ def tile_mom_e_kernel(
                         nc.tensor.transpose(
                             xt[:, jj, u, :], x_words[:, 2 * pair + jj, u : WIDTH // 2 : 2], ident_f32[:]
                         )
-                nc.vector.tensor_copy(
-                    out=g[:].bitcast(F32)[:, 2 * pair : 2 * pair + 2],
-                    in_=xt[:].rearrange("p j u t -> p j t u"),
-                )
+                dst = g[:].bitcast(F32)[:, 2 * pair : 2 * pair + 2]
+                src = xt[:].rearrange("p j u t -> p j t u")
+                if unit == 0 and pair == 1:
+                    nc.scalar.copy(out=dst, in_=src)
+                else:
+                    nc.vector.tensor_copy(out=dst, in_=src)
 
         def quantise_x(unit):
             c = x_stage.tile([P, TOKENS], U32, align_bytes=64)
@@ -233,9 +241,16 @@ def tile_mom_e_kernel(
             if unit < UNITS - FINE_STORES:
                 nc.sync.dma_start(out=out_dram[:, :, WIDTH * unit : WIDTH * (unit + 1)], in_=o[:])
 
+        def warm_up(count):
+            scrap = psum.tile([P, BANK], F32, tag="bank")
+            for rep in range(count):
+                nc.tensor.matmul(scrap[:], lhsT=warm[:, :P], rhs=warm[:], start=True, stop=True)
+
+        warm_up(4)
         transpose_x(0)
         quantise_x(0)
         per_feature_constants()
+        warm_up(2)
         transposed = 1
         transpose_x(1)
         quantised = 0

from contextlib import ExitStack

import concourse.mybir as mybir
from concourse.masks import make_identity

F32 = mybir.dt.float32
BF16 = mybir.dt.bfloat16
I32 = mybir.dt.int32
U32 = mybir.dt.uint32
U8 = mybir.dt.uint8
FP8X4 = mybir.dt.float8_e4m3fn_x4
FP4X4 = mybir.dt.float4_e2m1fn_x4
ACT = mybir.ActivationFunctionType
ALU = mybir.AluOpType

P = 128
TOKENS = 512
TOKEN_TILES = TOKENS // P
HEADS = 4
EXPERTS = 3
WIDTH = 512
UNITS = HEADS * EXPERTS
EPS = 1e-5

FEATURE_BLOCKS = WIDTH // P
BANK = 512

X_AHEAD = 2
FINE_STORES = 2

FLOPS = 2 * TOKENS * WIDTH * WIDTH * UNITS


def tile_mom_e_kernel(
    tc, x1, x2, x3, W_words, W_scales, b, gamma, beta, running_mean, running_var, out
):
    nc = tc.nc
    with ExitStack() as ctx:
        ctx.enter_context(tc.manual_schedule())
        const = ctx.enter_context(tc.tile_pool(name="const", bufs=1))
        x_stage = ctx.enter_context(tc.tile_pool(name="x_stage", bufs=5))
        z_pool = ctx.enter_context(tc.tile_pool(name="z_pool", bufs=4))
        out_pool = ctx.enter_context(tc.tile_pool(name="out_pool", bufs=4))
        psum = ctx.enter_context(tc.psum_pool(name="psum", bufs=8))

        xs = [x1, x2, x3]
        x_sb = []
        for unit in range(UNITS):
            x_tile = const.tile([P, TOKEN_TILES, WIDTH], BF16, name="x_sb%d" % unit)
            x_sb.append(x_tile)
        x_dram = [x.rearrange("(p j) k -> p j k", j=TOKEN_TILES) for x in xs]

        w_words = const.tile([P, EXPERTS, HEADS, 2 * WIDTH], U8, align_bytes=64)
        w_planes_first = const.tile([P, HEADS, WIDTH], U8, align_bytes=64)
        w_planes_rest = const.tile([P, EXPERTS - 1, HEADS, WIDTH], U8, align_bytes=64)
        w_planes = [w_planes_first[:], w_planes_rest[:, 0], w_planes_rest[:, 1]]
        w_words_dram = W_words.bitcast(I32).rearrange("(h e) p w -> e p h w", e=EXPERTS)
        w_scales_dram = W_scales.bitcast(I32).rearrange("(h e) (q r) n -> e r q h n", e=EXPERTS, r=4)

        vectors = [running_var, b, gamma, beta, running_mean]
        VECTOR_ROWS = 16
        ROW_BLOCKS = UNITS * FEATURE_BLOCKS // VECTOR_ROWS
        rows = const.tile([P, ROW_BLOCKS, P], BF16)
        warm = const.tile([P, BANK], BF16)
        nc.vector.memset(warm[:], 0.0)
        nc.vector.memset(rows[P // 2 : P], 0.0)
        nc.vector.memset(w_planes_first[:].rearrange("p h n -> p (h n)").bitcast(I32), 0)
        for v in range(len(vectors)):
            nc.scalar.dma_start(
                out=rows[VECTOR_ROWS * v : VECTOR_ROWS * (v + 1)].rearrange("p a c -> p (a c)"),
                in_=vectors[v]
                .rearrange("h e f -> h (e f)")
                .rearrange("h (q c) -> (h q) c", c=ROW_BLOCKS * P),
            )

        def load_x(unit):
            e, h = divmod(unit, HEADS)
            nc.sync.dma_start(out=x_sb[unit][:], in_=x_dram[e][:, :, WIDTH * h : WIDTH * (h + 1)])

        def load_weights(e, h0, h1):
            nc.sync.dma_start(
                out=w_words[:, e, h0:h1].bitcast(I32), in_=w_words_dram[e][:, h0:h1]
            )

        def load_scales(e):
            for r in range(4):
                nc.sync.dma_start(out=w_planes[e].bitcast(I32)[r:P:32], in_=w_scales_dram[e][r])

        table_probe = const.tile([P, 1], F32)
        nc.vector.memset(table_probe[:], 1.0)
        nc.scalar.activation(
            out=table_probe[:], in_=table_probe[:], func=ACT.Abs_reciprocal_sqrt, scale=1.0
        )
        ident_f32 = const.tile([P, P], F32)
        make_identity(nc, ident_f32[:])
        ident_bf16 = const.tile([P, P], BF16)
        make_identity(nc, ident_bf16[:])
        nc.gpsimd.memset(w_planes_rest[:].rearrange("p e h n -> p (e h n)").bitcast(I32), 0)

        load_x(0)
        load_x(1)
        load_weights(0, 0, 1)
        load_scales(0)
        load_x(2)
        load_weights(0, 1, HEADS)
        for unit in range(3, UNITS):
            load_x(unit)
            if unit > HEADS and unit % HEADS == 1:
                load_weights(unit // HEADS, 0, HEADS)
                load_scales(unit // HEADS)

        BLOCKS = UNITS * FEATURE_BLOCKS
        per_feature = const.tile([P, 4, VECTOR_ROWS, ROW_BLOCKS], F32)
        rstd = const.tile([P, VECTOR_ROWS, ROW_BLOCKS], F32)
        gain = const.tile([P, BLOCKS], F32)
        shift = const.tile([P, BLOCKS], F32)
        bias_t, gamma_t, beta_t, mean_t = [
            per_feature[:, v].rearrange("p q a -> p (q a)") for v in range(4)
        ]

        def per_feature_constants():
            rows_t = psum.tile([P, ROW_BLOCKS, P], BF16, tag="bank")
            for a in range(ROW_BLOCKS):
                nc.tensor.transpose(rows_t[:, a, :], rows[:, a, :], ident_bf16[:])
            nc.scalar.activation(
                out=rstd[:],
                in_=rows_t[:, :, 0:VECTOR_ROWS].rearrange("p a q -> p q a"),
                func=ACT.Abs_reciprocal_sqrt,
                bias=EPS,
                scale=1.0,
            )
            nc.scalar.copy(
                out=per_feature[:],
                in_=rows_t[:, :, VECTOR_ROWS : 5 * VECTOR_ROWS].rearrange("p a (v q) -> p v q a", v=4),
            )
            nc.scalar.activation(
                out=table_probe[:], in_=rstd[:, 0, 0:1], func=ACT.Gelu_apprx_sigmoid, scale=1.0
            )
            nc.gpsimd.tensor_mul(out=gain[:], in0=rstd[:].rearrange("p q a -> p (q a)"), in1=gamma_t)
            nc.gpsimd.tensor_mul(out=shift[:], in0=mean_t, in1=gain[:])
            nc.gpsimd.tensor_sub(out=shift[:], in0=beta_t, in1=shift[:])

        grouped = {}
        codes = {}
        x_planes = {}
        z_tiles = {}
        out_dram = out.rearrange("(p j) n -> p j n", j=TOKEN_TILES)

        def transpose_x(unit):
            x_words = x_sb[unit][:].bitcast(F32)
            g = x_stage.tile([P, TOKEN_TILES, P, 4], BF16, align_bytes=64)
            grouped[unit] = g
            for pair in range(TOKEN_TILES // 2):
                xt = psum.tile([P, 2, 2, P], F32, tag="bank")
                for jj in range(2):
                    for u in range(2):
                        nc.tensor.transpose(
                            xt[:, jj, u, :], x_words[:, 2 * pair + jj, u : WIDTH // 2 : 2], ident_f32[:]
                        )
                dst = g[:].bitcast(F32)[:, 2 * pair : 2 * pair + 2]
                src = xt[:].rearrange("p j u t -> p j t u")
                if unit == 0 and pair == 1:
                    nc.scalar.copy(out=dst, in_=src)
                else:
                    nc.vector.tensor_copy(out=dst, in_=src)

        def quantise_x(unit):
            c = x_stage.tile([P, TOKENS], U32, align_bytes=64)
            s = x_stage.tile([P, TOKENS], U8, align_bytes=64)
            codes[unit] = c
            x_planes[unit] = s
            nc.vector.quantize_mx(
                out=c[:].bitcast(FP8X4),
                scales=s[:],
                in_=grouped[unit][:].rearrange("p j t k -> p (j t k)"),
            )

        def multiply(unit):
            e, h = divmod(unit, HEADS)
            group = EXPERTS * h + e
            z = z_pool.tile([P, FEATURE_BLOCKS, TOKENS], F32)
            z_tiles[unit] = z
            accs = []
            for block in range(FEATURE_BLOCKS):
                acc = psum.tile([P, TOKENS], F32, tag="bank")
                accs.append(acc)
                nc.tensor.matmul_mx(
                    out=acc[:],
                    lhsT=w_words[:, e, h, 2 * P * block : 2 * P * (block + 1)].bitcast(FP4X4),
                    lhsT_scale=w_planes[e][:, h, P * block : P * (block + 1)],
                    rhs=codes[unit][:].bitcast(FP8X4),
                    rhs_scale=x_planes[unit][:],
                    start=True,
                    stop=True,
                )
            for block in range(FEATURE_BLOCKS):
                col = FEATURE_BLOCKS * group + block
                nc.scalar.activation(
                    out=z[:, block, :],
                    in_=accs[block][:],
                    func=ACT.Gelu_apprx_sigmoid,
                    bias=bias_t[:, col : col + 1],
                    scale=1.0,
                )
                engine = nc.vector if (block == 0 and unit % 2 == 1) else nc.gpsimd
                engine.tensor_scalar(
                    out=z[:, block, :],
                    in0=z[:, block, :],
                    scalar1=gain[:, col : col + 1],
                    scalar2=shift[:, col : col + 1],
                    op0=ALU.mult,
                    op1=ALU.add,
                )

        def transpose_out(unit):
            o = out_pool.tile([P, TOKEN_TILES, WIDTH], F32)
            z = z_tiles[unit]
            scalar_banks = (2, 3) if unit % 2 == 0 else (3,)
            for half in range(2):
                for pair in range(TOKEN_TILES // 2):
                    zt = psum.tile([P, 2, BANK // 2], F32, tag="bank")
                    for jj in range(2):
                        j = 2 * pair + jj
                        for i in range(2):
                            nc.tensor.transpose(
                                zt[:, jj, P * i : P * (i + 1)],
                                z[:, 2 * half + i, P * j : P * (j + 1)],
                                ident_f32[:],
                            )
                    dst = o[:, 2 * pair : 2 * pair + 2, (BANK // 2) * half : (BANK // 2) * (half + 1)]
                    if 2 * half + pair in scalar_banks:
                        nc.scalar.copy(out=dst, in_=zt[:])
                    else:
                        nc.vector.tensor_copy(out=dst, in_=zt[:])
                if unit >= UNITS - FINE_STORES:
                    first = (BANK // 2) * half
                    nc.sync.dma_start(
                        out=out_dram[:, :, WIDTH * unit + first : WIDTH * unit + first + BANK // 2],
                        in_=o[:, :, first : first + BANK // 2],
                    )
            if unit < UNITS - FINE_STORES:
                nc.sync.dma_start(out=out_dram[:, :, WIDTH * unit : WIDTH * (unit + 1)], in_=o[:])

        def warm_up(count):
            scrap = psum.tile([P, BANK], F32, tag="bank")
            for rep in range(count):
                nc.tensor.matmul(scrap[:], lhsT=warm[:, :P], rhs=warm[:], start=True, stop=True)

        warm_up(4)
        transpose_x(0)
        quantise_x(0)
        per_feature_constants()
        warm_up(2)
        transposed = 1
        transpose_x(1)
        quantised = 0
        for unit in range(UNITS):
            if quantised < min(unit + 1, transposed):
                quantised += 1
                quantise_x(quantised)
            multiply(unit)
            while transposed < min(unit + X_AHEAD, UNITS - 1):
                transposed += 1
                transpose_x(transposed)
                if quantised < min(unit + 1, transposed):
                    quantised += 1
                    quantise_x(quantised)
            if unit > 0:
                transpose_out(unit - 1)
        transpose_out(UNITS - 1)
